import numpy as np
import ml_dtypes


def mxq(x, axis, fmt="e4m3"):
    dtype, down = {"e4m3": (ml_dtypes.float8_e4m3fn, 7), "e5m2": (ml_dtypes.float8_e5m2, 14)}[fmt]
    v = np.moveaxis(np.asarray(x, np.float32).astype(ml_dtypes.bfloat16).astype(np.float64), axis, -1)
    blocks = v.reshape(v.shape[:-1] + (-1, 32))
    amax = np.abs(blocks).max(-1, keepdims=True)
    byte = np.maximum(np.where(amax > 0, np.frexp(amax)[1] - 1 + 127, 0) - down, 1)
    scale = np.exp2(byte - 127.0)
    codes = (blocks / scale).astype(np.float32).astype(dtype).astype(np.float64)
    return np.moveaxis((codes * scale).reshape(v.shape), -1, axis)


WIDE = False


def mx_kscale(k):
    if not WIDE:
        return np.ones(k)
    levels = np.array([10, -10, 5, -5, 0])
    a = np.random.permutation(np.resize(levels, k // 512 * 4)).reshape(k // 512, 4)
    idx = np.arange(k)
    return np.exp2(a[idx // 512, idx % 128 // 32])


BF16 = ml_dtypes.bfloat16


def bf(x):
    return np.asarray(x, np.float32).astype(BF16)


def f64(x):
    return np.asarray(x).astype(np.float64)


N, D, F, DEG = 1024, 512, 512, 32


def gcn_norm(adjacency):
    n = adjacency.shape[0]
    ahat = adjacency + np.eye(n)
    deg = ahat.sum(axis=0)
    dinv = np.where(deg > 0, deg ** -0.5, 0.0)
    return dinv[:, None] * ahat * dinv[None, :]


def setup_inputs():
    s = mx_kscale(D)
    adjacency = (np.random.uniform(size=(N, N)) < DEG / N) * (1.0 - np.eye(N))
    return {"x": bf(np.random.standard_normal((N, D)) * s),
            "adjacency": bf(adjacency),
            "w": bf(np.random.standard_normal((D, F)) * np.sqrt(DEG / D) / s[:, None]),
            "b": bf(np.random.standard_normal(F) * 0.3)}


def reference(x, adjacency, w, b):
    an = gcn_norm(f64(adjacency))
    xw = mxq(f64(x), 1, "e4m3") @ mxq(f64(w), 0, "e4m3")
    agg = mxq(an.T, 1, "e4m3") @ mxq(xw, 0, "e4m3")
    return np.maximum(agg + f64(b), 0.0)

@@ -1,0 +1,309 @@
+from contextlib import ExitStack
+
+import concourse.mybir as mybir
+from concourse.masks import make_identity
+
+F32 = mybir.dt.float32
+BF16 = mybir.dt.bfloat16
+U32 = mybir.dt.uint32
+U8 = mybir.dt.uint8
+FP8X4 = mybir.dt.float8_e4m3fn_x4
+ACT = mybir.ActivationFunctionType
+ALU = mybir.AluOpType
+AX = mybir.AxisListType
+
+P = 128
+N_NODES = 1024
+D_IN = 512
+F_OUT = 512
+NT = N_NODES // P
+RANGE = 256
+N_RANGES = N_NODES // RANGE
+HALVES = RANGE // P
+
+FLOPS = 2 * N_NODES * D_IN * F_OUT + 2 * N_NODES * N_NODES * F_OUT
+
+
+def tile_simplegcn_pa_kernel(tc, x, adjacency, w, b, out):
+    nc = tc.nc
+    with ExitStack() as ctx:
+        keep = ctx.enter_context(tc.tile_pool(name="keep", bufs=1))
+        ps_a = ctx.enter_context(tc.psum_pool(name="ps_a", bufs=4))
+        ps_b = ctx.enter_context(tc.psum_pool(name="ps_b", bufs=3))
+        ps_d = ctx.enter_context(tc.psum_pool(name="ps_d", bufs=1))
+        ctx.enter_context(tc.manual_schedule())
+
+        ident_f = keep.tile([P, P], F32, name="ident_f")
+        make_identity(nc, ident_f[:])
+        ident_b = keep.tile([P, P], BF16, name="ident_b")
+        make_identity(nc, ident_b[:])
+        ones_b = keep.tile([P, 8], BF16, name="ones_b")
+        nc.vector.memset(ones_b[:], 1.0)
+        warm_in = keep.tile([P, 1], F32, name="warm_in")
+        nc.vector.memset(warm_in[:], 1.0)
+        warm_out = keep.tile([P, 1], F32, name="warm_out")
+        nc.scalar.activation(out=warm_out[:], in_=warm_in[:], func=ACT.Sqrt)
+
+        w_sb = keep.tile([P, 4, F_OUT], BF16, name="w_sb")
+        nc.sync.dma_start(
+            out=w_sb[:].rearrange("p (u e) f -> p u e f", u=2),
+            in_=w.rearrange("(u p e) f -> p u e f", u=2, e=2),
+        )
+        x_sb = []
+        for c in range(2):
+            xh = keep.tile([P, 4, D_IN], BF16, name="x_sb%d" % c)
+            nc.sync.dma_start(
+                out=xh[:],
+                in_=x[c * 512 : (c + 1) * 512, :].rearrange("(s p) d -> p s d", p=P),
+            )
+            x_sb.append(xh)
+        adj = []
+        for k in range(NT):
+            ak = keep.tile([P, N_NODES], BF16, name="adj%d" % k)
+            nc.sync.dma_start(out=ak[:], in_=adjacency[k * P : (k + 1) * P, :])
+            adj.append(ak)
+        b_bc = keep.tile([P, F_OUT], BF16, name="b_bc")
+        nc.sync.dma_start(out=b_bc[:], in_=b.partition_broadcast(P))
+
+        wg = keep.tile([P, F_OUT, 4], BF16, name="wg", align_bytes=64)
+        nc.vector.tensor_copy(
+            out=wg[:].rearrange("p (c i) t -> p c t i", i=4),
+            in_=w_sb[:].rearrange("p t (c i) -> p c t i", i=4),
+        )
+        w_codes = keep.tile([P, F_OUT], U32, name="w_codes", align_bytes=64)
+        w_scales = keep.tile([P, F_OUT], U8, name="w_scales", align_bytes=64)
+        nc.vector.quantize_mx(
+            out=w_codes[:].bitcast(FP8X4),
+            scales=w_scales[:],
+            in_=wg[:].rearrange("p f t -> p (f t)"),
+        )
+
+        xg = keep.tile([P, NT * P * 4], BF16, name="xg", align_bytes=64)
+        xg32 = xg[:].bitcast(F32).rearrange("p (s n u) -> p s n u", s=NT, u=2)
+        x_codes = keep.tile([P, NT * P], U32, name="x_codes", align_bytes=64)
+        x_scales = keep.tile([P, NT * P], U8, name="x_scales", align_bytes=64)
+        for c in range(2):
+            for g in (2 * c, 2 * c + 1):
+                xt = ps_a.tile([P, 2, 2, P], F32, name="xt%d" % g, tag="A")
+                for a in range(2):
+                    s = 2 * g + a
+                    words = x_sb[s // 4][:, s % 4, :].bitcast(F32)
+                    for u in range(2):
+                        nc.tensor.transpose(
+                            xt[:, a, u, :], words[:, u * P : (u + 1) * P], ident_f[:]
+                        )
+                nc.scalar.copy(
+                    out=xg32[:, 2 * g : 2 * g + 2, :, :],
+                    in_=xt[:].rearrange("p a u n -> p a n u"),
+                )
+        for c in range(2):
+            nc.vector.quantize_mx(
+                out=x_codes[:, c * 512 : (c + 1) * 512].bitcast(FP8X4),
+                scales=x_scales[:, c * 512 : (c + 1) * 512],
+                in_=xg[:, c * 2048 : (c + 1) * 2048],
+            )
+
+        degp = ps_d.tile([P, (NT + 1) * NT], F32, name="degp")
+
+        def degree_part(k):
+            for m in range(NT):
+                nc.tensor.matmul(
+                    out=degp[:, k * NT + m : k * NT + m + 1],
+                    lhsT=adj[k][:, m * P : (m + 1) * P],
+                    rhs=ones_b[:, 0:1],
+                    start=True,
+                    stop=True,
+                )
+            nc.gpsimd.tensor_tensor(
+                out=adj[k][:, k * P : (k + 1) * P],
+                in0=adj[k][:, k * P : (k + 1) * P],
+                in1=ident_b[:],
+                op=ALU.add,
+            )
+
+        xwg = []
+        xw_codes = []
+        xw_scales = []
+        for c in range(2):
+            xwg.append(keep.tile([P, F_OUT, 4], BF16, name="xwg%d" % c, align_bytes=64))
+            xw_codes.append(
+                keep.tile([P, F_OUT], U32, name="xw_codes%d" % c, align_bytes=64)
+            )
+            xw_scales.append(
+                keep.tile([P, F_OUT], U8, name="xw_scales%d" % c, align_bytes=64)
+            )
+
+        def first_product(c):
+            for fc in range(4):
+                xwp = ps_b.tile([P, 4, P], F32, name="xwp%d_%d" % (c, fc), tag="B")
+                for t in range(4):
+                    s = 4 * c + t
+                    nc.tensor.matmul_mx(
+                        out=xwp[:, t, :],
+                        lhsT=x_codes[:, s * P : (s + 1) * P].bitcast(FP8X4),
+                        lhsT_scale=x_scales[:, s * P : (s + 1) * P],
+                        rhs=w_codes[:, fc * P : (fc + 1) * P].bitcast(FP8X4),
+                        rhs_scale=w_scales[:, fc * P : (fc + 1) * P],
+                        start=True,
+                        stop=True,
+                    )
+                nc.scalar.copy(
+                    out=xwg[c][:, fc * P : (fc + 1) * P, :],
+                    in_=xwp[:].rearrange("p t f -> p f t"),
+                )
+
+        def quantise_xw(c):
+            nc.vector.quantize_mx(
+                out=xw_codes[c][:].bitcast(FP8X4),
+                scales=xw_scales[c][:],
+                in_=xwg[c][:].rearrange("p f t -> p (f t)"),
+            )
+
+        degree_part(0)
+        first_product(0)
+        quantise_xw(0)
+        for k in (1, 2, 3):
+            degree_part(k)
+        first_product(1)
+        for k in (4, 5, 6, 7):
+            degree_part(k)
+        nc.tensor.matmul(
+            out=degp[:, NT * NT : (NT + 1) * NT],
+            lhsT=ident_b[:],
+            rhs=ones_b[:, 0:NT],
+            start=True,
+            stop=True,
+        )
+        deg = keep.tile([P, NT], F32, name="deg")
+        nc.vector.tensor_reduce(
+            out=deg[:],
+            in_=degp[:].rearrange("p (k m) -> p m k", m=NT),
+            axis=AX.X,
+            op=ALU.add,
+        )
+        rdeg = keep.tile([P, NT], F32, name="rdeg")
+        nc.vector.reciprocal(out=rdeg[:], in_=deg[:])
+        dinv = keep.tile([P, NT], F32, name="dinv")
+        nc.scalar.activation(out=dinv[:], in_=rdeg[:], func=ACT.Sqrt)
+        quantise_xw(1)
+
+        dbc = []
+        v = []
+        ang = []
+        a_codes = []
+        a_scales = []
+        for r in range(N_RANGES):
+            d = ps_a.tile([P, RANGE], F32, name="dbc%d" % r, tag="A")
+            for h in range(HALVES):
+                m = r * HALVES + h
+                nc.tensor.transpose(
+                    d[:, h * P : (h + 1) * P],
+                    dinv[:, m : m + 1].to_broadcast([P, P]),
+                    ident_f[:],
+                )
+            dbc.append(d)
+            v.append(keep.tile([P, NT, RANGE], F32, name="v%d" % r))
+            ang.append(
+                keep.tile([P, 2, RANGE, 4], BF16, name="ang%d" % r, align_bytes=64)
+            )
+            a_codes.append(
+                keep.tile([P, 2 * RANGE], U32, name="a_codes%d" % r, align_bytes=64)
+            )
+            a_scales.append(
+                keep.tile([P, 2 * RANGE], U8, name="a_scales%d" % r, align_bytes=64)
+            )
+
+        def scale_rows(r, c):
+            for s in range(4 * c, 4 * c + 4):
+                nc.scalar.activation(
+                    out=v[r][:, s, :],
+                    in_=adj[s][:, r * RANGE : (r + 1) * RANGE],
+                    func=ACT.Copy,
+                    scale=dinv[:, s : s + 1],
+                )
+
+        def scale_cols(r, c):
+            nc.vector.tensor_tensor(
+                out=ang[r][:, c, :, :],
+                in0=v[r][:, 4 * c : 4 * c + 4, :].rearrange("p t j -> p j t"),
+                in1=dbc[r][:].unsqueeze(2).to_broadcast([P, RANGE, 4]),
+                op=ALU.mult,
+            )
+
+        def quantise_an(r):
+            nc.vector.quantize_mx(
+                out=a_codes[r][:].bitcast(FP8X4),
+                scales=a_scales[r][:],
+                in_=ang[r][:].rearrange("p c j t -> p (c j t)"),
+            )
+
+        acc = {}
+        res = {}
+
+        def second_product(r):
+            for h in range(HALVES):
+                a = ps_b.tile([P, F_OUT], F32, name="acc%d_%d" % (r, h), tag="B")
+                for c in range(2):
+                    lo = c * RANGE + h * P
+                    nc.tensor.matmul_mx(
+                        out=a[:],
+                        lhsT=a_codes[r][:, lo : lo + P].bitcast(FP8X4),
+                        lhsT_scale=a_scales[r][:, lo : lo + P],
+                        rhs=xw_codes[c][:].bitcast(FP8X4),
+                        rhs_scale=xw_scales[c][:],
+                        start=(c == 0),
+                        stop=(c == 1),
+                    )
+                acc[(r, h)] = a
+
+        def add_bias(r, h):
+            t = keep.tile([P, F_OUT], F32, name="res%d_%d" % (r, h))
+            nc.vector.tensor_tensor(out=t[:], in0=acc[(r, h)][:], in1=b_bc[:], op=ALU.add)
+            res[(r, h)] = t
+
+        def relu_store(r, h):
+            t = res[(r, h)]
+            nc.scalar.activation(out=t[:], in_=t[:], func=ACT.Relu)
+            row = r * RANGE + h * P
+            nc.sync.dma_start(out=out[row : row + P, :], in_=t[:])
+
+        scale_rows(0, 0)
+        scale_rows(0, 1)
+        scale_cols(0, 0)
+        scale_cols(0, 1)
+        scale_rows(1, 0)
+        scale_rows(1, 1)
+        scale_cols(1, 0)
+        quantise_an(0)
+        second_product(0)
+        scale_cols(1, 1)
+        scale_rows(2, 0)
+        scale_rows(2, 1)
+        scale_cols(2, 0)
+        quantise_an(1)
+        second_product(1)
+        add_bias(0, 0)
+        add_bias(0, 1)
+        scale_rows(3, 0)
+        relu_store(0, 0)
+        relu_store(0, 1)
+        scale_rows(3, 1)
+        scale_cols(2, 1)
+        scale_cols(3, 0)
+        quantise_an(2)
+        second_product(2)
+        add_bias(1, 0)
+        add_bias(1, 1)
+        relu_store(1, 0)
+        relu_store(1, 1)
+        scale_cols(3, 1)
+        add_bias(2, 0)
+        quantise_an(3)
+        second_product(3)
+        add_bias(2, 1)
+        relu_store(2, 0)
+        relu_store(2, 1)
+        add_bias(3, 0)
+        add_bias(3, 1)
+        relu_store(3, 0)
+        relu_store(3, 1)

@@ -7,6 +7,7 @@ F32 = mybir.dt.float32
 BF16 = mybir.dt.bfloat16
 U32 = mybir.dt.uint32
 U8 = mybir.dt.uint8
+I32 = mybir.dt.int32
 FP8X4 = mybir.dt.float8_e4m3fn_x4
 ACT = mybir.ActivationFunctionType
 ALU = mybir.AluOpType
@@ -20,6 +21,8 @@ NT = N_NODES // P
 RANGE = 256
 N_RANGES = N_NODES // RANGE
 HALVES = RANGE // P
+WARM_A = 8
+WARM_B = 2
 
 FLOPS = 2 * N_NODES * D_IN * F_OUT + 2 * N_NODES * N_NODES * F_OUT
 
@@ -43,6 +46,29 @@ def tile_simplegcn_pa_kernel(tc, x, adjacency, w, b, out):
         nc.vector.memset(warm_in[:], 1.0)
         warm_out = keep.tile([P, 1], F32, name="warm_out")
         nc.scalar.activation(out=warm_out[:], in_=warm_in[:], func=ACT.Sqrt)
+
+        zero_bf = keep.tile([P, 2048], BF16, name="zero_bf", align_bytes=64)
+        nc.vector.memset(zero_bf[:].bitcast(I32), 0)
+        zero_codes = keep.tile([P, 512], U32, name="zero_codes", align_bytes=64)
+        zero_scales = keep.tile([P, 512], U8, name="zero_scales", align_bytes=64)
+        nc.vector.quantize_mx(
+            out=zero_codes[:].bitcast(FP8X4), scales=zero_scales[:], in_=zero_bf[:]
+        )
+
+        def keep_clock_up(tag, count):
+            scratch = ps_b.tile([P, 512], F32, name="scratch%s" % tag, tag="B")
+            for i in range(count):
+                nc.tensor.matmul_mx(
+                    out=scratch[:],
+                    lhsT=zero_codes[:, 0:P].bitcast(FP8X4),
+                    lhsT_scale=zero_scales[:, 0:P],
+                    rhs=zero_codes[:].bitcast(FP8X4),
+                    rhs_scale=zero_scales[:],
+                    start=True,
+                    stop=True,
+                )
+
+        keep_clock_up("a", WARM_A)
 
         w_sb = keep.tile([P, 4, F_OUT], BF16, name="w_sb")
         nc.sync.dma_start(
@@ -96,6 +122,7 @@ def tile_simplegcn_pa_kernel(tc, x, adjacency, w, b, out):
                     out=xg32[:, 2 * g : 2 * g + 2, :, :],
                     in_=xt[:].rearrange("p a u n -> p a n u"),
                 )
+            keep_clock_up("b%d" % c, WARM_B)
         for c in range(2):
             nc.vector.quantize_mx(
                 out=x_codes[:, c * 512 : (c + 1) * 512].bitcast(FP8X4),

@@ -7,7 +7,6 @@ F32 = mybir.dt.float32
 BF16 = mybir.dt.bfloat16
 U32 = mybir.dt.uint32
 U8 = mybir.dt.uint8
-I32 = mybir.dt.int32
 FP8X4 = mybir.dt.float8_e4m3fn_x4
 ACT = mybir.ActivationFunctionType
 ALU = mybir.AluOpType
@@ -21,8 +20,6 @@ NT = N_NODES // P
 RANGE = 256
 N_RANGES = N_NODES // RANGE
 HALVES = RANGE // P
-WARM_A = 8
-WARM_B = 2
 
 FLOPS = 2 * N_NODES * D_IN * F_OUT + 2 * N_NODES * N_NODES * F_OUT
 
@@ -46,29 +43,6 @@ def tile_simplegcn_pa_kernel(tc, x, adjacency, w, b, out):
         nc.vector.memset(warm_in[:], 1.0)
         warm_out = keep.tile([P, 1], F32, name="warm_out")
         nc.scalar.activation(out=warm_out[:], in_=warm_in[:], func=ACT.Sqrt)
-
-        zero_bf = keep.tile([P, 2048], BF16, name="zero_bf", align_bytes=64)
-        nc.vector.memset(zero_bf[:].bitcast(I32), 0)
-        zero_codes = keep.tile([P, 512], U32, name="zero_codes", align_bytes=64)
-        zero_scales = keep.tile([P, 512], U8, name="zero_scales", align_bytes=64)
-        nc.vector.quantize_mx(
-            out=zero_codes[:].bitcast(FP8X4), scales=zero_scales[:], in_=zero_bf[:]
-        )
-
-        def keep_clock_up(tag, count):
-            scratch = ps_b.tile([P, 512], F32, name="scratch%s" % tag, tag="B")
-            for i in range(count):
-                nc.tensor.matmul_mx(
-                    out=scratch[:],
-                    lhsT=zero_codes[:, 0:P].bitcast(FP8X4),
-                    lhsT_scale=zero_scales[:, 0:P],
-                    rhs=zero_codes[:].bitcast(FP8X4),
-                    rhs_scale=zero_scales[:],
-                    start=True,
-                    stop=True,
-                )
-
-        keep_clock_up("a", WARM_A)
 
         w_sb = keep.tile([P, 4, F_OUT], BF16, name="w_sb")
         nc.sync.dma_start(
@@ -122,7 +96,6 @@ def tile_simplegcn_pa_kernel(tc, x, adjacency, w, b, out):
                     out=xg32[:, 2 * g : 2 * g + 2, :, :],
                     in_=xt[:].rearrange("p a u n -> p a n u"),
                 )
-            keep_clock_up("b%d" % c, WARM_B)
         for c in range(2):
             nc.vector.quantize_mx(
                 out=x_codes[:, c * 512 : (c + 1) * 512].bitcast(FP8X4),
@@ -251,9 +224,12 @@ def tile_simplegcn_pa_kernel(tc, x, adjacency, w, b, out):
 
         def scale_cols(r, c):
             nc.vector.tensor_tensor(
-                out=ang[r][:, c, :, :],
-                in0=v[r][:, 4 * c : 4 * c + 4, :].rearrange("p t j -> p j t"),
-                in1=dbc[r][:].unsqueeze(2).to_broadcast([P, RANGE, 4]),
+                out=ang[r][:, c, :, :].rearrange("p (g i) t -> p g t i", i=4),
+                in0=v[r][:, 4 * c : 4 * c + 4, :].rearrange("p t (g i) -> p g t i", i=4),
+                in1=dbc[r][:]
+                .rearrange("p (g i) -> p g i", i=4)
+                .unsqueeze(2)
+                .to_broadcast([P, RANGE // 4, 4, 4]),
                 op=ALU.mult,
             )
 

@@ -50,11 +50,11 @@ def tile_simplegcn_pa_kernel(tc, x, adjacency, w, b, out):
             in_=w.rearrange("(u p e) f -> p u e f", u=2, e=2),
         )
         x_sb = []
-        for c in range(2):
-            xh = keep.tile([P, 4, D_IN], BF16, name="x_sb%d" % c)
+        for g in range(NT // 2):
+            xh = keep.tile([P, 2, D_IN], BF16, name="x_sb%d" % g)
             nc.sync.dma_start(
                 out=xh[:],
-                in_=x[c * 512 : (c + 1) * 512, :].rearrange("(s p) d -> p s d", p=P),
+                in_=x[g * 256 : (g + 1) * 256, :].rearrange("(a p) d -> p a d", p=P),
             )
             x_sb.append(xh)
         adj = []
@@ -82,20 +82,18 @@ def tile_simplegcn_pa_kernel(tc, x, adjacency, w, b, out):
         xg32 = xg[:].bitcast(F32).rearrange("p (s n u) -> p s n u", s=NT, u=2)
         x_codes = keep.tile([P, NT * P], U32, name="x_codes", align_bytes=64)
         x_scales = keep.tile([P, NT * P], U8, name="x_scales", align_bytes=64)
-        for c in range(2):
-            for g in (2 * c, 2 * c + 1):
-                xt = ps_a.tile([P, 2, 2, P], F32, name="xt%d" % g, tag="A")
-                for a in range(2):
-                    s = 2 * g + a
-                    words = x_sb[s // 4][:, s % 4, :].bitcast(F32)
-                    for u in range(2):
-                        nc.tensor.transpose(
-                            xt[:, a, u, :], words[:, u * P : (u + 1) * P], ident_f[:]
-                        )
-                nc.scalar.copy(
-                    out=xg32[:, 2 * g : 2 * g + 2, :, :],
-                    in_=xt[:].rearrange("p a u n -> p a n u"),
-                )
+        for g in range(NT // 2):
+            xt = ps_a.tile([P, 2, 2, P], F32, name="xt%d" % g, tag="A")
+            for a in range(2):
+                words = x_sb[g][:, a, :].bitcast(F32)
+                for u in range(2):
+                    nc.tensor.transpose(
+                        xt[:, a, u, :], words[:, u * P : (u + 1) * P], ident_f[:]
+                    )
+            nc.scalar.copy(
+                out=xg32[:, 2 * g : 2 * g + 2, :, :],
+                in_=xt[:].rearrange("p a u n -> p a n u"),
+            )
         for c in range(2):
             nc.vector.quantize_mx(
                 out=x_codes[:, c * 512 : (c + 1) * 512].bitcast(FP8X4),
@@ -132,25 +130,28 @@ def tile_simplegcn_pa_kernel(tc, x, adjacency, w, b, out):
             xw_scales.append(
                 keep.tile([P, F_OUT], U8, name="xw_scales%d" % c, align_bytes=64)
             )
+        xwp = {}
 
-        def first_product(c):
-            for fc in range(4):
-                xwp = ps_b.tile([P, 4, P], F32, name="xwp%d_%d" % (c, fc), tag="B")
-                for t in range(4):
-                    s = 4 * c + t
-                    nc.tensor.matmul_mx(
-                        out=xwp[:, t, :],
-                        lhsT=x_codes[:, s * P : (s + 1) * P].bitcast(FP8X4),
-                        lhsT_scale=x_scales[:, s * P : (s + 1) * P],
-                        rhs=w_codes[:, fc * P : (fc + 1) * P].bitcast(FP8X4),
-                        rhs_scale=w_scales[:, fc * P : (fc + 1) * P],
-                        start=True,
-                        stop=True,
-                    )
-                nc.scalar.copy(
-                    out=xwg[c][:, fc * P : (fc + 1) * P, :],
-                    in_=xwp[:].rearrange("p t f -> p f t"),
+        def first_product(c, fc):
+            bank = ps_b.tile([P, 4, P], F32, name="xwp%d_%d" % (c, fc), tag="B")
+            for t in range(4):
+                s = 4 * c + t
+                nc.tensor.matmul_mx(
+                    out=bank[:, t, :],
+                    lhsT=x_codes[:, s * P : (s + 1) * P].bitcast(FP8X4),
+                    lhsT_scale=x_scales[:, s * P : (s + 1) * P],
+                    rhs=w_codes[:, fc * P : (fc + 1) * P].bitcast(FP8X4),
+                    rhs_scale=w_scales[:, fc * P : (fc + 1) * P],
+                    start=True,
+                    stop=True,
                 )
+            xwp[(c, fc)] = bank
+
+        def empty_bank(c, fc, engine_copy):
+            engine_copy(
+                out=xwg[c][:, fc * P : (fc + 1) * P, :],
+                in_=xwp[(c, fc)][:].rearrange("p t f -> p f t"),
+            )
 
         def quantise_xw(c):
             nc.vector.quantize_mx(
@@ -159,21 +160,22 @@ def tile_simplegcn_pa_kernel(tc, x, adjacency, w, b, out):
                 in_=xwg[c][:].rearrange("p f t -> p (f t)"),
             )
 
-        degree_part(0)
-        first_product(0)
-        quantise_xw(0)
-        for k in (1, 2, 3):
+        for k in range(NT):
             degree_part(k)
-        first_product(1)
-        for k in (4, 5, 6, 7):
-            degree_part(k)
-        nc.tensor.matmul(
-            out=degp[:, NT * NT : (NT + 1) * NT],
-            lhsT=ident_b[:],
-            rhs=ones_b[:, 0:NT],
-            start=True,
-            stop=True,
-        )
+            if k == NT - 1:
+                nc.tensor.matmul(
+                    out=degp[:, NT * NT : (NT + 1) * NT],
+                    lhsT=ident_b[:],
+                    rhs=ones_b[:, 0:NT],
+                    start=True,
+                    stop=True,
+                )
+            first_product(k // 4, k % 4)
+            if k < NT - 1:
+                empty_bank(k // 4, k % 4, nc.scalar.copy)
+            if k == 3:
+                quantise_xw(0)
+
         deg = keep.tile([P, NT], F32, name="deg")
         nc.vector.tensor_reduce(
             out=deg[:],
@@ -185,7 +187,7 @@ def tile_simplegcn_pa_kernel(tc, x, adjacency, w, b, out):
         nc.vector.reciprocal(out=rdeg[:], in_=deg[:])
         dinv = keep.tile([P, NT], F32, name="dinv")
         nc.scalar.activation(out=dinv[:], in_=rdeg[:], func=ACT.Sqrt)
-        quantise_xw(1)
+        empty_bank(1, 3, nc.vector.tensor_copy)
 
         dbc = []
         v = []
@@ -213,14 +215,20 @@ def tile_simplegcn_pa_kernel(tc, x, adjacency, w, b, out):
                 keep.tile([P, 2 * RANGE], U8, name="a_scales%d" % r, align_bytes=64)
             )
 
+        def scale_row_tile(r, s, on_vector=False):
+            src = adj[s][:, r * RANGE : (r + 1) * RANGE]
+            if on_vector:
+                nc.vector.tensor_scalar_mul(
+                    out=v[r][:, s, :], in0=src, scalar1=dinv[:, s : s + 1]
+                )
+            else:
+                nc.scalar.activation(
+                    out=v[r][:, s, :], in_=src, func=ACT.Copy, scale=dinv[:, s : s + 1]
+                )
+
         def scale_rows(r, c):
             for s in range(4 * c, 4 * c + 4):
-                nc.scalar.activation(
-                    out=v[r][:, s, :],
-                    in_=adj[s][:, r * RANGE : (r + 1) * RANGE],
-                    func=ACT.Copy,
-                    scale=dinv[:, s : s + 1],
-                )
+                scale_row_tile(r, s)
 
         def scale_cols(r, c):
             nc.vector.tensor_tensor(
@@ -270,7 +278,11 @@ def tile_simplegcn_pa_kernel(tc, x, adjacency, w, b, out):
             row = r * RANGE + h * P
             nc.sync.dma_start(out=out[row : row + P, :], in_=t[:])
 
-        scale_rows(0, 0)
+        scale_row_tile(0, 0)
+        scale_row_tile(0, 1)
+        scale_row_tile(0, 2, on_vector=True)
+        scale_row_tile(0, 3, on_vector=True)
+        quantise_xw(1)
         scale_rows(0, 1)
         scale_cols(0, 0)
         scale_cols(0, 1)

@@ -28,8 +28,8 @@ def tile_simplegcn_pa_kernel(tc, x, adjacency, w, b, out):
     nc = tc.nc
     with ExitStack() as ctx:
         keep = ctx.enter_context(tc.tile_pool(name="keep", bufs=1))
-        ps_a = ctx.enter_context(tc.psum_pool(name="ps_a", bufs=4))
-        ps_b = ctx.enter_context(tc.psum_pool(name="ps_b", bufs=3))
+        ps_a = ctx.enter_context(tc.psum_pool(name="ps_a", bufs=2))
+        ps_b = ctx.enter_context(tc.psum_pool(name="ps_b", bufs=5))
         ps_d = ctx.enter_context(tc.psum_pool(name="ps_d", bufs=1))
         ctx.enter_context(tc.manual_schedule())
 
@@ -42,7 +42,9 @@ def tile_simplegcn_pa_kernel(tc, x, adjacency, w, b, out):
         warm_in = keep.tile([P, 1], F32, name="warm_in")
         nc.vector.memset(warm_in[:], 1.0)
         warm_out = keep.tile([P, 1], F32, name="warm_out")
-        nc.scalar.activation(out=warm_out[:], in_=warm_in[:], func=ACT.Sqrt)
+        nc.scalar.activation(
+            out=warm_out[:], in_=warm_in[:], func=ACT.Abs_reciprocal_sqrt
+        )
 
         w_sb = keep.tile([P, 4, F_OUT], BF16, name="w_sb")
         nc.sync.dma_start(
@@ -62,6 +64,9 @@ def tile_simplegcn_pa_kernel(tc, x, adjacency, w, b, out):
             ak = keep.tile([P, N_NODES], BF16, name="adj%d" % k)
             nc.sync.dma_start(out=ak[:], in_=adjacency[k * P : (k + 1) * P, :])
             adj.append(ak)
+        b_rows = keep.tile([P, P], BF16, name="b_rows")
+        nc.gpsimd.memset(b_rows[:], 0.0)
+        nc.sync.dma_start(out=b_rows[0:4, :], in_=b.rearrange("(r c) -> r c", c=P))
         b_bc = keep.tile([P, F_OUT], BF16, name="b_bc")
         nc.sync.dma_start(out=b_bc[:], in_=b.partition_broadcast(P))
 
@@ -101,7 +106,7 @@ def tile_simplegcn_pa_kernel(tc, x, adjacency, w, b, out):
                 in_=xg[:, c * 2048 : (c + 1) * 2048],
             )
 
-        degp = ps_d.tile([P, (NT + 1) * NT], F32, name="degp")
+        degp = ps_d.tile([P, (NT + 1) * NT], F32, name="degp", tag="D")
 
         def degree_part(k):
             for m in range(NT):
@@ -183,10 +188,8 @@ def tile_simplegcn_pa_kernel(tc, x, adjacency, w, b, out):
             axis=AX.X,
             op=ALU.add,
         )
-        rdeg = keep.tile([P, NT], F32, name="rdeg")
-        nc.vector.reciprocal(out=rdeg[:], in_=deg[:])
         dinv = keep.tile([P, NT], F32, name="dinv")
-        nc.scalar.activation(out=dinv[:], in_=rdeg[:], func=ACT.Sqrt)
+        nc.scalar.activation(out=dinv[:], in_=deg[:], func=ACT.Abs_reciprocal_sqrt)
         empty_bank(1, 3, nc.vector.tensor_copy)
 
         dbc = []
@@ -194,16 +197,21 @@ def tile_simplegcn_pa_kernel(tc, x, adjacency, w, b, out):
         ang = []
         a_codes = []
         a_scales = []
-        for r in range(N_RANGES):
-            d = ps_a.tile([P, RANGE], F32, name="dbc%d" % r, tag="A")
-            for h in range(HALVES):
-                m = r * HALVES + h
+        for pair in range(N_RANGES // 2):
+            d = ps_a.tile([P, 2 * RANGE], F32, name="dbc%d" % pair, tag="A")
+            for q in range(2 * HALVES):
+                m = pair * 2 * HALVES + q
                 nc.tensor.transpose(
-                    d[:, h * P : (h + 1) * P],
+                    d[:, q * P : (q + 1) * P],
                     dinv[:, m : m + 1].to_broadcast([P, P]),
                     ident_f[:],
                 )
-            dbc.append(d)
+            dbc.append(d[:, 0:RANGE])
+            dbc.append(d[:, RANGE : 2 * RANGE])
+        b_t = ps_d.tile([P, P], BF16, name="b_t", tag="D")
+        nc.tensor.transpose(b_t[:], b_rows[:], ident_b[:])
+        b_col = keep.tile([P, 4], F32, name="b_col")
+        for r in range(N_RANGES):
             v.append(keep.tile([P, NT, RANGE], F32, name="v%d" % r))
             ang.append(
                 keep.tile([P, 2, RANGE, 4], BF16, name="ang%d" % r, align_bytes=64)
@@ -234,7 +242,7 @@ def tile_simplegcn_pa_kernel(tc, x, adjacency, w, b, out):
             nc.vector.tensor_tensor(
                 out=ang[r][:, c, :, :].rearrange("p (g i) t -> p g t i", i=4),
                 in0=v[r][:, 4 * c : 4 * c + 4, :].rearrange("p t (g i) -> p g t i", i=4),
-                in1=dbc[r][:]
+                in1=dbc[r]
                 .rearrange("p (g i) -> p g i", i=4)
                 .unsqueeze(2)
                 .to_broadcast([P, RANGE // 4, 4, 4]),
@@ -267,14 +275,68 @@ def tile_simplegcn_pa_kernel(tc, x, adjacency, w, b, out):
                     )
                 acc[(r, h)] = a
 
-        def add_bias(r, h):
-            t = keep.tile([P, F_OUT], F32, name="res%d_%d" % (r, h))
-            nc.vector.tensor_tensor(out=t[:], in0=acc[(r, h)][:], in1=b_bc[:], op=ALU.add)
-            res[(r, h)] = t
+        def add_bias(r, h, lo=0, hi=F_OUT):
+            if (r, h) not in res:
+                res[(r, h)] = keep.tile([P, F_OUT], F32, name="res%d_%d" % (r, h))
+            nc.vector.tensor_tensor(
+                out=res[(r, h)][:, lo:hi],
+                in0=acc[(r, h)][:, lo:hi],
+                in1=b_bc[:, lo:hi],
+                op=ALU.add,
+            )
 
-        def relu_store(r, h):
+        def relu_store(r, h, lo=0, hi=F_OUT):
             t = res[(r, h)]
-            nc.scalar.activation(out=t[:], in_=t[:], func=ACT.Relu)
+            nc.scalar.activation(out=t[:, lo:hi], in_=t[:, lo:hi], func=ACT.Relu)
+            row = r * RANGE + h * P
+            nc.sync.dma_start(out=out[row : row + P, lo:hi], in_=t[:, lo:hi])
+
+        acc_t = {}
+        out_t = {}
+        back = {}
+
+        def second_product_transposed(r):
+            for half in range(2):
+                bank = ps_b.tile([P, 2, RANGE], F32, name="acct%d_%d" % (r, half), tag="B")
+                for q in range(2):
+                    ft = 2 * half + q
+                    for c in range(2):
+                        nc.tensor.matmul_mx(
+                            out=bank[:, q, :],
+                            lhsT=xw_codes[c][:, ft * P : (ft + 1) * P].bitcast(FP8X4),
+                            lhsT_scale=xw_scales[c][:, ft * P : (ft + 1) * P],
+                            rhs=a_codes[r][:, c * RANGE : (c + 1) * RANGE].bitcast(FP8X4),
+                            rhs_scale=a_scales[r][:, c * RANGE : (c + 1) * RANGE],
+                            start=(c == 0),
+                            stop=(c == 1),
+                        )
+                acc_t[(r, half)] = bank
+
+        def relu_bias(r):
+            t = keep.tile([P, 4, RANGE], F32, name="out_t%d" % r)
+            for ft in range(4):
+                nc.scalar.activation(
+                    out=t[:, ft, :],
+                    in_=acc_t[(r, ft // 2)][:, ft % 2, :],
+                    func=ACT.Relu,
+                    bias=b_col[:, ft : ft + 1],
+                    scale=1.0,
+                )
+            out_t[r] = t
+
+        def transpose_back(r, h):
+            bank = ps_b.tile([P, F_OUT], F32, name="back%d_%d" % (r, h), tag="B")
+            for ft in range(4):
+                nc.tensor.transpose(
+                    bank[:, ft * P : (ft + 1) * P],
+                    out_t[r][:, ft, h * P : (h + 1) * P],
+                    ident_f[:],
+                )
+            back[(r, h)] = bank
+
+        def copy_store(r, h):
+            t = keep.tile([P, F_OUT], F32, name="res%d_%d" % (r, h))
+            nc.scalar.copy(out=t[:], in_=back[(r, h)][:])
             row = r * RANGE + h * P
             nc.sync.dma_start(out=out[row : row + P, :], in_=t[:])
 
@@ -290,27 +352,30 @@ def tile_simplegcn_pa_kernel(tc, x, adjacency, w, b, out):
         scale_rows(1, 1)
         scale_cols(1, 0)
         quantise_an(0)
-        second_product(0)
+        second_product_transposed(0)
         scale_cols(1, 1)
         scale_rows(2, 0)
         scale_rows(2, 1)
         scale_cols(2, 0)
         quantise_an(1)
-        second_product(1)
-        add_bias(0, 0)
-        add_bias(0, 1)
+        second_product_transposed(1)
+        nc.scalar.copy(out=b_col[:], in_=b_t[:, 0:4])
+        relu_bias(0)
+        transpose_back(0, 0)
+        transpose_back(0, 1)
         scale_rows(3, 0)
-        relu_store(0, 0)
-        relu_store(0, 1)
         scale_rows(3, 1)
         scale_cols(2, 1)
         scale_cols(3, 0)
         quantise_an(2)
         second_product(2)
-        add_bias(1, 0)
-        add_bias(1, 1)
-        relu_store(1, 0)
-        relu_store(1, 1)
+        relu_bias(1)
+        transpose_back(1, 0)
+        transpose_back(1, 1)
+        copy_store(0, 0)
+        copy_store(0, 1)
+        copy_store(1, 0)
+        copy_store(1, 1)
         scale_cols(3, 1)
         add_bias(2, 0)
         quantise_an(3)
@@ -319,6 +384,8 @@ def tile_simplegcn_pa_kernel(tc, x, adjacency, w, b, out):
         relu_store(2, 0)
         relu_store(2, 1)
         add_bias(3, 0)
-        add_bias(3, 1)
+        add_bias(3, 1, 0, 256)
+        add_bias(3, 1, 256, 512)
         relu_store(3, 0)
-        relu_store(3, 1)
+        relu_store(3, 1, 0, 256)
+        relu_store(3, 1, 256, 512)

@@ -358,7 +358,7 @@ def tile_simplegcn_pa_kernel(tc, x, adjacency, w, b, out):
         scale_rows(2, 1)
         scale_cols(2, 0)
         quantise_an(1)
-        second_product_transposed(1)
+        second_product(1)
         nc.scalar.copy(out=b_col[:], in_=b_t[:, 0:4])
         relu_bias(0)
         transpose_back(0, 0)
@@ -366,16 +366,15 @@ def tile_simplegcn_pa_kernel(tc, x, adjacency, w, b, out):
         scale_rows(3, 0)
         scale_rows(3, 1)
         scale_cols(2, 1)
+        add_bias(1, 0)
+        add_bias(1, 1)
         scale_cols(3, 0)
         quantise_an(2)
         second_product(2)
-        relu_bias(1)
-        transpose_back(1, 0)
-        transpose_back(1, 1)
         copy_store(0, 0)
         copy_store(0, 1)
-        copy_store(1, 0)
-        copy_store(1, 1)
+        relu_store(1, 0)
+        relu_store(1, 1)
         scale_cols(3, 1)
         add_bias(2, 0)
         quantise_an(3)

@@ -234,9 +234,21 @@ def tile_simplegcn_pa_kernel(tc, x, adjacency, w, b, out):
                     out=v[r][:, s, :], in_=src, func=ACT.Copy, scale=dinv[:, s : s + 1]
                 )
 
+        gate = keep.tile([P, 1], F32, name="gate")
+
         def scale_rows(r, c):
-            for s in range(4 * c, 4 * c + 4):
+            for s in range(4 * c, 4 * c + (4 if r == 0 else 3)):
                 scale_row_tile(r, s)
+
+        def scale_row_tile_gpsimd(r, s):
+            nc.gpsimd.tensor_scalar(
+                out=v[r][:, s, :],
+                in0=adj[s][:, r * RANGE : (r + 1) * RANGE],
+                scalar1=dinv[:, s : s + 1],
+                scalar2=gate[:, 0:1],
+                op0=ALU.mult,
+                op1=ALU.add,
+            )
 
         def scale_cols(r, c):
             nc.vector.tensor_tensor(
@@ -345,6 +357,10 @@ def tile_simplegcn_pa_kernel(tc, x, adjacency, w, b, out):
         scale_row_tile(0, 2, on_vector=True)
         scale_row_tile(0, 3, on_vector=True)
         quantise_xw(1)
+        nc.vector.memset(gate[:], 0.0)
+        for r in (1, 2, 3):
+            scale_row_tile_gpsimd(r, 3)
+            scale_row_tile_gpsimd(r, 7)
         scale_rows(0, 1)
         scale_cols(0, 0)
         scale_cols(0, 1)
@@ -358,7 +374,7 @@ def tile_simplegcn_pa_kernel(tc, x, adjacency, w, b, out):
         scale_rows(2, 1)
         scale_cols(2, 0)
         quantise_an(1)
-        second_product(1)
+        second_product_transposed(1)
         nc.scalar.copy(out=b_col[:], in_=b_t[:, 0:4])
         relu_bias(0)
         transpose_back(0, 0)
@@ -366,15 +382,16 @@ def tile_simplegcn_pa_kernel(tc, x, adjacency, w, b, out):
         scale_rows(3, 0)
         scale_rows(3, 1)
         scale_cols(2, 1)
-        add_bias(1, 0)
-        add_bias(1, 1)
         scale_cols(3, 0)
         quantise_an(2)
         second_product(2)
+        relu_bias(1)
+        transpose_back(1, 0)
+        transpose_back(1, 1)
         copy_store(0, 0)
         copy_store(0, 1)
-        relu_store(1, 0)
-        relu_store(1, 1)
+        copy_store(1, 0)
+        copy_store(1, 1)
         scale_cols(3, 1)
         add_bias(2, 0)
         quantise_an(3)

from contextlib import ExitStack

import concourse.mybir as mybir
from concourse.masks import make_identity

F32 = mybir.dt.float32
BF16 = mybir.dt.bfloat16
U32 = mybir.dt.uint32
U8 = mybir.dt.uint8
FP8X4 = mybir.dt.float8_e4m3fn_x4
ACT = mybir.ActivationFunctionType
ALU = mybir.AluOpType
AX = mybir.AxisListType

P = 128
N_NODES = 1024
D_IN = 512
F_OUT = 512
NT = N_NODES // P
RANGE = 256
N_RANGES = N_NODES // RANGE
HALVES = RANGE // P

FLOPS = 2 * N_NODES * D_IN * F_OUT + 2 * N_NODES * N_NODES * F_OUT


def tile_simplegcn_pa_kernel(tc, x, adjacency, w, b, out):
    nc = tc.nc
    with ExitStack() as ctx:
        keep = ctx.enter_context(tc.tile_pool(name="keep", bufs=1))
        ps_a = ctx.enter_context(tc.psum_pool(name="ps_a", bufs=2))
        ps_b = ctx.enter_context(tc.psum_pool(name="ps_b", bufs=5))
        ps_d = ctx.enter_context(tc.psum_pool(name="ps_d", bufs=1))
        ctx.enter_context(tc.manual_schedule())

        ident_f = keep.tile([P, P], F32, name="ident_f")
        make_identity(nc, ident_f[:])
        ident_b = keep.tile([P, P], BF16, name="ident_b")
        make_identity(nc, ident_b[:])
        ones_b = keep.tile([P, 8], BF16, name="ones_b")
        nc.vector.memset(ones_b[:], 1.0)
        warm_in = keep.tile([P, 1], F32, name="warm_in")
        nc.vector.memset(warm_in[:], 1.0)
        warm_out = keep.tile([P, 1], F32, name="warm_out")
        nc.scalar.activation(
            out=warm_out[:], in_=warm_in[:], func=ACT.Abs_reciprocal_sqrt
        )

        w_sb = keep.tile([P, 4, F_OUT], BF16, name="w_sb")
        nc.sync.dma_start(
            out=w_sb[:].rearrange("p (u e) f -> p u e f", u=2),
            in_=w.rearrange("(u p e) f -> p u e f", u=2, e=2),
        )
        x_sb = []
        for g in range(NT // 2):
            xh = keep.tile([P, 2, D_IN], BF16, name="x_sb%d" % g)
            nc.sync.dma_start(
                out=xh[:],
                in_=x[g * 256 : (g + 1) * 256, :].rearrange("(a p) d -> p a d", p=P),
            )
            x_sb.append(xh)
        adj = []
        for k in range(NT):
            ak = keep.tile([P, N_NODES], BF16, name="adj%d" % k)
            nc.sync.dma_start(out=ak[:], in_=adjacency[k * P : (k + 1) * P, :])
            adj.append(ak)
        b_rows = keep.tile([P, P], BF16, name="b_rows")
        nc.gpsimd.memset(b_rows[:], 0.0)
        nc.sync.dma_start(out=b_rows[0:4, :], in_=b.rearrange("(r c) -> r c", c=P))
        b_bc = keep.tile([P, F_OUT], BF16, name="b_bc")
        nc.sync.dma_start(out=b_bc[:], in_=b.partition_broadcast(P))

        wg = keep.tile([P, F_OUT, 4], BF16, name="wg", align_bytes=64)
        nc.vector.tensor_copy(
            out=wg[:].rearrange("p (c i) t -> p c t i", i=4),
            in_=w_sb[:].rearrange("p t (c i) -> p c t i", i=4),
        )
        w_codes = keep.tile([P, F_OUT], U32, name="w_codes", align_bytes=64)
        w_scales = keep.tile([P, F_OUT], U8, name="w_scales", align_bytes=64)
        nc.vector.quantize_mx(
            out=w_codes[:].bitcast(FP8X4),
            scales=w_scales[:],
            in_=wg[:].rearrange("p f t -> p (f t)"),
        )

        xg = keep.tile([P, NT * P * 4], BF16, name="xg", align_bytes=64)
        xg32 = xg[:].bitcast(F32).rearrange("p (s n u) -> p s n u", s=NT, u=2)
        x_codes = keep.tile([P, NT * P], U32, name="x_codes", align_bytes=64)
        x_scales = keep.tile([P, NT * P], U8, name="x_scales", align_bytes=64)
        for g in range(NT // 2):
            xt = ps_a.tile([P, 2, 2, P], F32, name="xt%d" % g, tag="A")
            for a in range(2):
                words = x_sb[g][:, a, :].bitcast(F32)
                for u in range(2):
                    nc.tensor.transpose(
                        xt[:, a, u, :], words[:, u * P : (u + 1) * P], ident_f[:]
                    )
            nc.scalar.copy(
                out=xg32[:, 2 * g : 2 * g + 2, :, :],
                in_=xt[:].rearrange("p a u n -> p a n u"),
            )
        for c in range(2):
            nc.vector.quantize_mx(
                out=x_codes[:, c * 512 : (c + 1) * 512].bitcast(FP8X4),
                scales=x_scales[:, c * 512 : (c + 1) * 512],
                in_=xg[:, c * 2048 : (c + 1) * 2048],
            )

        degp = ps_d.tile([P, (NT + 1) * NT], F32, name="degp", tag="D")

        def degree_part(k):
            for m in range(NT):
                nc.tensor.matmul(
                    out=degp[:, k * NT + m : k * NT + m + 1],
                    lhsT=adj[k][:, m * P : (m + 1) * P],
                    rhs=ones_b[:, 0:1],
                    start=True,
                    stop=True,
                )
            nc.gpsimd.tensor_tensor(
                out=adj[k][:, k * P : (k + 1) * P],
                in0=adj[k][:, k * P : (k + 1) * P],
                in1=ident_b[:],
                op=ALU.add,
            )

        xwg = []
        xw_codes = []
        xw_scales = []
        for c in range(2):
            xwg.append(keep.tile([P, F_OUT, 4], BF16, name="xwg%d" % c, align_bytes=64))
            xw_codes.append(
                keep.tile([P, F_OUT], U32, name="xw_codes%d" % c, align_bytes=64)
            )
            xw_scales.append(
                keep.tile([P, F_OUT], U8, name="xw_scales%d" % c, align_bytes=64)
            )
        xwp = {}

        def first_product(c, fc):
            bank = ps_b.tile([P, 4, P], F32, name="xwp%d_%d" % (c, fc), tag="B")
            for t in range(4):
                s = 4 * c + t
                nc.tensor.matmul_mx(
                    out=bank[:, t, :],
                    lhsT=x_codes[:, s * P : (s + 1) * P].bitcast(FP8X4),
                    lhsT_scale=x_scales[:, s * P : (s + 1) * P],
                    rhs=w_codes[:, fc * P : (fc + 1) * P].bitcast(FP8X4),
                    rhs_scale=w_scales[:, fc * P : (fc + 1) * P],
                    start=True,
                    stop=True,
                )
            xwp[(c, fc)] = bank

        def empty_bank(c, fc, engine_copy):
            engine_copy(
                out=xwg[c][:, fc * P : (fc + 1) * P, :],
                in_=xwp[(c, fc)][:].rearrange("p t f -> p f t"),
            )

        def quantise_xw(c):
            nc.vector.quantize_mx(
                out=xw_codes[c][:].bitcast(FP8X4),
                scales=xw_scales[c][:],
                in_=xwg[c][:].rearrange("p f t -> p (f t)"),
            )

        for k in range(NT):
            degree_part(k)
            if k == NT - 1:
                nc.tensor.matmul(
                    out=degp[:, NT * NT : (NT + 1) * NT],
                    lhsT=ident_b[:],
                    rhs=ones_b[:, 0:NT],
                    start=True,
                    stop=True,
                )
            first_product(k // 4, k % 4)
            if k < NT - 1:
                empty_bank(k // 4, k % 4, nc.scalar.copy)
            if k == 3:
                quantise_xw(0)

        deg = keep.tile([P, NT], F32, name="deg")
        nc.vector.tensor_reduce(
            out=deg[:],
            in_=degp[:].rearrange("p (k m) -> p m k", m=NT),
            axis=AX.X,
            op=ALU.add,
        )
        dinv = keep.tile([P, NT], F32, name="dinv")
        nc.scalar.activation(out=dinv[:], in_=deg[:], func=ACT.Abs_reciprocal_sqrt)
        empty_bank(1, 3, nc.vector.tensor_copy)

        dbc = []
        v = []
        ang = []
        a_codes = []
        a_scales = []
        for pair in range(N_RANGES // 2):
            d = ps_a.tile([P, 2 * RANGE], F32, name="dbc%d" % pair, tag="A")
            for q in range(2 * HALVES):
                m = pair * 2 * HALVES + q
                nc.tensor.transpose(
                    d[:, q * P : (q + 1) * P],
                    dinv[:, m : m + 1].to_broadcast([P, P]),
                    ident_f[:],
                )
            dbc.append(d[:, 0:RANGE])
            dbc.append(d[:, RANGE : 2 * RANGE])
        b_t = ps_d.tile([P, P], BF16, name="b_t", tag="D")
        nc.tensor.transpose(b_t[:], b_rows[:], ident_b[:])
        b_col = keep.tile([P, 4], F32, name="b_col")
        for r in range(N_RANGES):
            v.append(keep.tile([P, NT, RANGE], F32, name="v%d" % r))
            ang.append(
                keep.tile([P, 2, RANGE, 4], BF16, name="ang%d" % r, align_bytes=64)
            )
            a_codes.append(
                keep.tile([P, 2 * RANGE], U32, name="a_codes%d" % r, align_bytes=64)
            )
            a_scales.append(
                keep.tile([P, 2 * RANGE], U8, name="a_scales%d" % r, align_bytes=64)
            )

        def scale_row_tile(r, s, on_vector=False):
            src = adj[s][:, r * RANGE : (r + 1) * RANGE]
            if on_vector:
                nc.vector.tensor_scalar_mul(
                    out=v[r][:, s, :], in0=src, scalar1=dinv[:, s : s + 1]
                )
            else:
                nc.scalar.activation(
                    out=v[r][:, s, :], in_=src, func=ACT.Copy, scale=dinv[:, s : s + 1]
                )

        gate = keep.tile([P, 1], F32, name="gate")

        def scale_rows(r, c):
            for s in range(4 * c, 4 * c + (4 if r == 0 else 3)):
                scale_row_tile(r, s)

        def scale_row_tile_gpsimd(r, s):
            nc.gpsimd.tensor_scalar(
                out=v[r][:, s, :],
                in0=adj[s][:, r * RANGE : (r + 1) * RANGE],
                scalar1=dinv[:, s : s + 1],
                scalar2=gate[:, 0:1],
                op0=ALU.mult,
                op1=ALU.add,
            )

        def scale_cols(r, c):
            nc.vector.tensor_tensor(
                out=ang[r][:, c, :, :].rearrange("p (g i) t -> p g t i", i=4),
                in0=v[r][:, 4 * c : 4 * c + 4, :].rearrange("p t (g i) -> p g t i", i=4),
                in1=dbc[r]
                .rearrange("p (g i) -> p g i", i=4)
                .unsqueeze(2)
                .to_broadcast([P, RANGE // 4, 4, 4]),
                op=ALU.mult,
            )

        def quantise_an(r):
            nc.vector.quantize_mx(
                out=a_codes[r][:].bitcast(FP8X4),
                scales=a_scales[r][:],
                in_=ang[r][:].rearrange("p c j t -> p (c j t)"),
            )

        acc = {}
        res = {}

        def second_product(r):
            for h in range(HALVES):
                a = ps_b.tile([P, F_OUT], F32, name="acc%d_%d" % (r, h), tag="B")
                for c in range(2):
                    lo = c * RANGE + h * P
                    nc.tensor.matmul_mx(
                        out=a[:],
                        lhsT=a_codes[r][:, lo : lo + P].bitcast(FP8X4),
                        lhsT_scale=a_scales[r][:, lo : lo + P],
                        rhs=xw_codes[c][:].bitcast(FP8X4),
                        rhs_scale=xw_scales[c][:],
                        start=(c == 0),
                        stop=(c == 1),
                    )
                acc[(r, h)] = a

        def add_bias(r, h, lo=0, hi=F_OUT):
            if (r, h) not in res:
                res[(r, h)] = keep.tile([P, F_OUT], F32, name="res%d_%d" % (r, h))
            nc.vector.tensor_tensor(
                out=res[(r, h)][:, lo:hi],
                in0=acc[(r, h)][:, lo:hi],
                in1=b_bc[:, lo:hi],
                op=ALU.add,
            )

        def relu_store(r, h, lo=0, hi=F_OUT):
            t = res[(r, h)]
            nc.scalar.activation(out=t[:, lo:hi], in_=t[:, lo:hi], func=ACT.Relu)
            row = r * RANGE + h * P
            nc.sync.dma_start(out=out[row : row + P, lo:hi], in_=t[:, lo:hi])

        acc_t = {}
        out_t = {}
        back = {}

        def second_product_transposed(r):
            for half in range(2):
                bank = ps_b.tile([P, 2, RANGE], F32, name="acct%d_%d" % (r, half), tag="B")
                for q in range(2):
                    ft = 2 * half + q
                    for c in range(2):
                        nc.tensor.matmul_mx(
                            out=bank[:, q, :],
                            lhsT=xw_codes[c][:, ft * P : (ft + 1) * P].bitcast(FP8X4),
                            lhsT_scale=xw_scales[c][:, ft * P : (ft + 1) * P],
                            rhs=a_codes[r][:, c * RANGE : (c + 1) * RANGE].bitcast(FP8X4),
                            rhs_scale=a_scales[r][:, c * RANGE : (c + 1) * RANGE],
                            start=(c == 0),
                            stop=(c == 1),
                        )
                acc_t[(r, half)] = bank

        def relu_bias(r):
            t = keep.tile([P, 4, RANGE], F32, name="out_t%d" % r)
            for ft in range(4):
                nc.scalar.activation(
                    out=t[:, ft, :],
                    in_=acc_t[(r, ft // 2)][:, ft % 2, :],
                    func=ACT.Relu,
                    bias=b_col[:, ft : ft + 1],
                    scale=1.0,
                )
            out_t[r] = t

        def transpose_back(r, h):
            bank = ps_b.tile([P, F_OUT], F32, name="back%d_%d" % (r, h), tag="B")
            for ft in range(4):
                nc.tensor.transpose(
                    bank[:, ft * P : (ft + 1) * P],
                    out_t[r][:, ft, h * P : (h + 1) * P],
                    ident_f[:],
                )
            back[(r, h)] = bank

        def copy_store(r, h):
            t = keep.tile([P, F_OUT], F32, name="res%d_%d" % (r, h))
            nc.scalar.copy(out=t[:], in_=back[(r, h)][:])
            row = r * RANGE + h * P
            nc.sync.dma_start(out=out[row : row + P, :], in_=t[:])

        scale_row_tile(0, 0)
        scale_row_tile(0, 1)
        scale_row_tile(0, 2, on_vector=True)
        scale_row_tile(0, 3, on_vector=True)
        quantise_xw(1)
        nc.vector.memset(gate[:], 0.0)
        for r in (1, 2, 3):
            scale_row_tile_gpsimd(r, 3)
            scale_row_tile_gpsimd(r, 7)
        scale_rows(0, 1)
        scale_cols(0, 0)
        scale_cols(0, 1)
        scale_rows(1, 0)
        scale_rows(1, 1)
        scale_cols(1, 0)
        quantise_an(0)
        second_product_transposed(0)
        scale_cols(1, 1)
        scale_rows(2, 0)
        scale_rows(2, 1)
        scale_cols(2, 0)
        quantise_an(1)
        second_product_transposed(1)
        nc.scalar.copy(out=b_col[:], in_=b_t[:, 0:4])
        relu_bias(0)
        transpose_back(0, 0)
        transpose_back(0, 1)
        scale_rows(3, 0)
        scale_rows(3, 1)
        scale_cols(2, 1)
        scale_cols(3, 0)
        quantise_an(2)
        second_product(2)
        relu_bias(1)
        transpose_back(1, 0)
        transpose_back(1, 1)
        copy_store(0, 0)
        copy_store(0, 1)
        copy_store(1, 0)
        copy_store(1, 1)
        scale_cols(3, 1)
        add_bias(2, 0)
        quantise_an(3)
        second_product(3)
        add_bias(2, 1)
        relu_store(2, 0)
        relu_store(2, 1)
        add_bias(3, 0)
        add_bias(3, 1, 0, 256)
        add_bias(3, 1, 256, 512)
        relu_store(3, 0)
        relu_store(3, 1, 0, 256)
        relu_store(3, 1, 256, 512)
